import numpy as np
import ml_dtypes


def mxq(x, axis, fmt="e4m3"):
    dtype, down = {"e4m3": (ml_dtypes.float8_e4m3fn, 7), "e5m2": (ml_dtypes.float8_e5m2, 14)}[fmt]
    v = np.moveaxis(np.asarray(x, np.float32).astype(ml_dtypes.bfloat16).astype(np.float64), axis, -1)
    blocks = v.reshape(v.shape[:-1] + (-1, 32))
    amax = np.abs(blocks).max(-1, keepdims=True)
    byte = np.maximum(np.where(amax > 0, np.frexp(amax)[1] - 1 + 127, 0) - down, 1)
    scale = np.exp2(byte - 127.0)
    codes = (blocks / scale).astype(np.float32).astype(dtype).astype(np.float64)
    return np.moveaxis((codes * scale).reshape(v.shape), -1, axis)


WIDE = False


def mx_kscale(k):
    if not WIDE:
        return np.ones(k)
    levels = np.array([10, -10, 5, -5, 0])
    if k % 512:
        return np.exp2(np.random.permutation(np.resize(levels, k // 32))).repeat(32)
    a = np.empty((k // 512, 16))
    for p in range(k // 512):
        a[p, :8] = np.random.permutation(np.resize(levels, 8))
        for g in range(8):
            far = levels[np.abs(levels - a[p, g]) >= 10]
            a[p, g + 8] = far[np.random.randint(len(far))]
    return np.exp2(a.ravel()).repeat(32)


BF16 = ml_dtypes.bfloat16


def bf(x):
    return np.asarray(x, np.float32).astype(BF16)


def f64(x):
    return np.asarray(x).astype(np.float64)


B, N, K, H, NUM_IN = 4, 64, 30, 512, 512


def setup_inputs():
    s, t = mx_kscale(H), mx_kscale(H)
    u = np.random.standard_normal((B, N, H))
    e = np.random.standard_normal((B, N, K, H))
    return {"h1": bf(np.maximum((u[:, :, None, :] + e) * 0.7, 0.0) * s),
            "h_V": bf(np.random.standard_normal((B, N, H))),
            "mask_attend": bf(np.random.random((B, N, K)) < 0.9),
            "W2": bf(np.random.standard_normal((H, H)) * 1.4 / np.sqrt(H) / s[:, None] * t),
            "b2": bf(np.random.standard_normal(H) * 0.2 * t),
            "W3": bf(np.random.standard_normal((H, H)) * 2.8 / np.sqrt(H) / t[:, None]),
            "b3": bf(np.random.standard_normal(H) * 0.2)}


def reference(h1, h_V, mask_attend, W2, b2, W3, b3):
    h2 = np.maximum((mxq(f64(h1), 3, "e4m3") @ mxq(f64(W2), 0, "e4m3")) + f64(b2), 0.0)
    msg = ((mxq(h2, 3, "e4m3") @ mxq(f64(W3), 0, "e4m3")) + f64(b3)) * f64(mask_attend)[..., None]
    return f64(h_V) + np.mean(msg, axis=-2)

@@ -1,0 +1,290 @@
+from contextlib import ExitStack
+
+import concourse.mybir as mybir
+from concourse.masks import make_identity
+
+F32 = mybir.dt.float32
+BF16 = mybir.dt.bfloat16
+U32 = mybir.dt.uint32
+U8 = mybir.dt.uint8
+FP8X4 = mybir.dt.float8_e4m3fn_x4
+ALU = mybir.AluOpType
+ACT = mybir.ActivationFunctionType
+
+P = 128
+PACK = 4
+HID = 512
+WORDS = HID // 2
+SLOTS = 30
+NODE_BLOCKS = 2
+SLOTS_PER_ROUND = 2
+TILES = NODE_BLOCKS * SLOTS_PER_ROUND
+COLS = TILES * P
+ROUNDS = SLOTS // SLOTS_PER_ROUND
+
+LAG_LAYER1 = 1
+LAG_REGROUP = 2
+LAG_LAYER2 = 3
+STEP_OF_W3 = 0
+STEP_OF_BASE = ROUNDS - 1
+LAST_ROUND_PIECES = NODE_BLOCKS
+
+FLOPS = 2 * 2 * (NODE_BLOCKS * P * SLOTS) * HID * HID
+
+
+def tile_mpnnlayer_pb_kernel(tc, h1, h_V, mask_attend, W2, b2, W3, b3, out):
+    nc = tc.nc
+    h1_rows = h1.rearrange("b n k h -> (b n) (k h)")
+    hv_rows = h_V.rearrange("b n h -> (b n) h")
+    mask_rows = mask_attend.rearrange("b n k -> (b n) k")
+    out_rows = out.rearrange("b n h -> (b n) h")
+
+    with ExitStack() as ctx:
+        ctx.enter_context(tc.manual_schedule())
+        keep = ctx.enter_context(tc.tile_pool(name="keep", bufs=1))
+        work = ctx.enter_context(tc.tile_pool(name="work", bufs=3))
+        psum = ctx.enter_context(tc.psum_pool(name="psum", bufs=1))
+
+        h1_sb = [keep.tile([P, SLOTS * HID], BF16, name="h1_sb%d" % nb) for nb in range(NODE_BLOCKS)]
+
+        def load_h1(r):
+            cols = slice(r * SLOTS_PER_ROUND * HID, (r + 1) * SLOTS_PER_ROUND * HID)
+            for nb in range(NODE_BLOCKS):
+                nc.sync.dma_start(out=h1_sb[nb][:, cols], in_=h1_rows[nb * P : (nb + 1) * P, cols])
+
+        mask_bf = keep.tile([P, NODE_BLOCKS, SLOTS], BF16)
+        nc.sync.dma_start(out=mask_bf[:], in_=mask_rows.rearrange("(nb q) k -> q nb k", q=P))
+        w2_raw = keep.tile([P, PACK, HID], BF16)
+        nc.sync.dma_start(out=w2_raw[:], in_=W2.rearrange("(p t) f -> p t f", t=PACK))
+        b2_bf = keep.tile([P, PACK], BF16)
+        nc.sync.dma_start(out=b2_bf[:], in_=b2.rearrange("(p t) -> p t", t=PACK))
+        load_h1(0)
+        load_h1(1)
+        w3_raw = keep.tile([P, PACK, HID], BF16)
+        nc.sync.dma_start(out=w3_raw[:], in_=W3.rearrange("(p t) f -> p t f", t=PACK))
+        for r in range(2, ROUNDS):
+            load_h1(r)
+        b3_all = keep.tile([P, HID], BF16)
+        nc.sync.dma_start(out=b3_all[:], in_=b3.partition_broadcast(P))
+        hv = keep.tile([P, NODE_BLOCKS, HID], BF16)
+        nc.sync.dma_start(out=hv[:], in_=hv_rows.rearrange("(nb q) h -> q nb h", q=P))
+
+        ident = keep.tile([P, P], F32)
+        make_identity(nc, ident[:])
+        mask_f = keep.tile([P, ROUNDS, NODE_BLOCKS, SLOTS_PER_ROUND], F32)
+        nc.vector.tensor_copy(out=mask_f[:], in_=mask_bf[:].rearrange("q nb (r s) -> q r nb s", s=SLOTS_PER_ROUND))
+        h1_words = [h1_sb[nb][:].bitcast(F32) for nb in range(NODE_BLOCKS)]
+        diags = {}
+        banks = {}
+        h1_q = {}
+        hiddens = {}
+        h2_q = {}
+
+        def build_diags(r):
+            diag = work.tile([P, TILES, P], F32)
+            nc.vector.tensor_tensor(
+                out=diag[:],
+                in0=ident[:].unsqueeze(1).to_broadcast([P, TILES, P]),
+                in1=mask_f[:, r, :, :].rearrange("q nb s -> q (nb s)").unsqueeze(2).to_broadcast([P, TILES, P]),
+                op=ALU.mult,
+            )
+            diags[r] = diag
+
+        def transpose_h1(r):
+            banks[r] = []
+            for nb in range(NODE_BLOCKS):
+                bank = psum.tile([P, 2, SLOTS_PER_ROUND * P], F32, name="xt%d" % nb)
+                for s in range(SLOTS_PER_ROUND):
+                    for u in range(2):
+                        first = (r * SLOTS_PER_ROUND + s) * WORDS
+                        nc.tensor.transpose(
+                            bank[:, u, s * P : (s + 1) * P],
+                            h1_words[nb][:, first + u : first + WORDS : 2],
+                            diags[r][:, nb * SLOTS_PER_ROUND + s, :],
+                        )
+                banks[r].append(bank)
+
+        def group_h1(r):
+            h1_grouped = work.tile([P, COLS * PACK], BF16, align_bytes=64)
+            grouped_words = h1_grouped[:].bitcast(F32).rearrange("p (c u) -> p c u", u=2)
+            for nb in range(NODE_BLOCKS):
+                nc.scalar.copy(
+                    out=grouped_words[:, nb * SLOTS_PER_ROUND * P : (nb + 1) * SLOTS_PER_ROUND * P, :],
+                    in_=banks[r][nb][:].rearrange("p u c -> p c u"),
+                )
+            return h1_grouped
+
+        def quantise_h1(r, h1_grouped):
+            h1_codes = work.tile([P, COLS], U32, align_bytes=64)
+            h1_scales = work.tile([P, COLS], U8, align_bytes=64)
+            nc.vector.quantize_mx(out=h1_codes[:].bitcast(FP8X4), scales=h1_scales[:], in_=h1_grouped[:])
+            h1_q[r] = (h1_codes, h1_scales)
+
+        def pieces_of(r):
+            return LAST_ROUND_PIECES if r == ROUNDS - 1 else 1
+
+        def piece_cols(r, piece):
+            width = COLS // pieces_of(r)
+            return slice(piece * width, (piece + 1) * width)
+
+        w2_codes = keep.tile([P, HID], U32, align_bytes=64)
+        w2_scales = keep.tile([P, HID], U8, align_bytes=64)
+        b2_f = keep.tile([P, PACK], F32)
+
+        def prepare_w2():
+            nc.vector.tensor_copy(out=b2_f[:], in_=b2_bf[:])
+            w2_grouped = keep.tile([P, HID, PACK], BF16, align_bytes=64)
+            nc.vector.tensor_copy(
+                out=w2_grouped[:].rearrange("p (t2 c) t -> p t2 c t", t2=PACK),
+                in_=w2_raw[:].rearrange("p t (c t2) -> p t2 c t", t2=PACK),
+            )
+            nc.vector.quantize_mx(
+                out=w2_codes[:].bitcast(FP8X4), scales=w2_scales[:], in_=w2_grouped[:].rearrange("p c t -> p (c t)")
+            )
+
+        def layer1(r):
+            codes, scales = h1_q[r]
+            hidden = work.tile([P, PACK, COLS], BF16)
+            x_banks = [psum.tile([P, COLS], F32, name="x%d" % t2) for t2 in range(PACK)]
+            for piece in range(pieces_of(r)):
+                cols = piece_cols(r, piece)
+                for t2 in range(PACK):
+                    nc.tensor.matmul_mx(
+                        out=x_banks[t2][:, cols],
+                        lhsT=w2_codes[:, t2 * P : (t2 + 1) * P].bitcast(FP8X4),
+                        lhsT_scale=w2_scales[:, t2 * P : (t2 + 1) * P],
+                        rhs=codes[:, cols].bitcast(FP8X4),
+                        rhs_scale=scales[:, cols],
+                        start=True,
+                        stop=True,
+                    )
+                    nc.scalar.activation(
+                        out=hidden[:, t2, cols], in_=x_banks[t2][:, cols], func=ACT.Relu, bias=b2_f[:, t2 : t2 + 1], scale=1.0
+                    )
+            hiddens[r] = hidden
+
+        def regroup_h2(r, h2_grouped, piece):
+            cols = piece_cols(r, piece)
+            nc.vector.tensor_copy(
+                out=h2_grouped[:, cols, :].rearrange("p (c i) t -> p c t i", i=4),
+                in_=hiddens[r][:, :, cols].rearrange("p t (c i) -> p c t i", i=4),
+            )
+
+        w3_codes = keep.tile([P, HID], U32, align_bytes=64)
+        w3_scales = keep.tile([P, HID], U8, align_bytes=64)
+
+        def prepare_w3():
+            w3_grouped = keep.tile([P, HID, PACK], BF16, align_bytes=64)
+            nc.vector.tensor_copy(out=w3_grouped[:], in_=w3_raw[:].rearrange("p t f -> p f t"))
+            nc.vector.quantize_mx(
+                out=w3_codes[:].bitcast(FP8X4), scales=w3_scales[:], in_=w3_grouped[:].rearrange("p f t -> p (f t)")
+            )
+
+        base = keep.tile([P, NODE_BLOCKS, HID], F32)
+
+        def prepare_base():
+            idle_grouped = keep.tile([P, P, PACK], BF16, align_bytes=64)
+            nc.vector.tensor_scalar(
+                out=idle_grouped[:],
+                in0=b2_f[:].unsqueeze(1).to_broadcast([P, P, PACK]),
+                scalar1=0.0,
+                scalar2=None,
+                op0=ALU.max,
+            )
+            count = keep.tile([P, NODE_BLOCKS], F32)
+            nc.vector.reduce_sum(out=count[:], in_=mask_f[:].rearrange("q r nb s -> q nb r s"), axis=mybir.AxisListType.XY)
+            idle_codes = keep.tile([P, P], U32, align_bytes=64)
+            idle_scales = keep.tile([P, P], U8, align_bytes=64)
+            nc.vector.quantize_mx(
+                out=idle_codes[:].bitcast(FP8X4), scales=idle_scales[:], in_=idle_grouped[:].rearrange("p c t -> p (c t)")
+            )
+            idle_ps = psum.tile([P, HID], F32, name="xt0")
+            nc.tensor.matmul_mx(
+                out=idle_ps[:],
+                lhsT=idle_codes[:].bitcast(FP8X4),
+                lhsT_scale=idle_scales[:],
+                rhs=w3_codes[:].bitcast(FP8X4),
+                rhs_scale=w3_scales[:],
+                start=True,
+                stop=True,
+            )
+            kept_share = keep.tile([P, NODE_BLOCKS], F32)
+            nc.vector.tensor_scalar(out=kept_share[:], in0=count[:], scalar1=1.0 / SLOTS, scalar2=None, op0=ALU.mult)
+            minus_masked_share = keep.tile([P, NODE_BLOCKS], F32)
+            nc.vector.tensor_scalar(
+                out=minus_masked_share[:], in0=count[:], scalar1=1.0 / SLOTS, scalar2=-1.0, op0=ALU.mult, op1=ALU.add
+            )
+            for nb in range(NODE_BLOCKS):
+                nc.vector.scalar_tensor_tensor(
+                    out=base[:, nb, :], in0=b3_all[:], scalar=kept_share[:, nb : nb + 1], in1=hv[:, nb, :],
+                    op0=ALU.mult, op1=ALU.add,
+                )
+            for nb in range(NODE_BLOCKS):
+                nc.vector.scalar_tensor_tensor(
+                    out=base[:, nb, :], in0=idle_ps[:], scalar=minus_masked_share[:, nb : nb + 1], in1=base[:, nb, :],
+                    op0=ALU.mult, op1=ALU.add,
+                )
+
+        acc = [psum.tile([P, HID], F32, name="acc%d" % nb) for nb in range(NODE_BLOCKS)]
+
+        def quantise_h2(r, h2_grouped):
+            h2_codes = work.tile([P, COLS], U32, align_bytes=64)
+            h2_scales = work.tile([P, COLS], U8, align_bytes=64)
+            for piece in range(pieces_of(r)):
+                cols = piece_cols(r, piece)
+                nc.vector.quantize_mx(
+                    out=h2_codes[:, cols].bitcast(FP8X4),
+                    scales=h2_scales[:, cols],
+                    in_=h2_grouped[:, cols, :].rearrange("p c t -> p (c t)"),
+                )
+            h2_q[r] = (h2_codes, h2_scales)
+
+        def layer2(r):
+            h2_codes, h2_scales = h2_q[r]
+            for tile_i in range(TILES):
+                slot = r * SLOTS_PER_ROUND + tile_i % SLOTS_PER_ROUND
+                nc.tensor.matmul_mx(
+                    out=acc[tile_i // SLOTS_PER_ROUND][:],
+                    lhsT=h2_codes[:, tile_i * P : (tile_i + 1) * P].bitcast(FP8X4),
+                    lhsT_scale=h2_scales[:, tile_i * P : (tile_i + 1) * P],
+                    rhs=w3_codes[:].bitcast(FP8X4),
+                    rhs_scale=w3_scales[:],
+                    start=(slot == 0),
+                    stop=(slot == SLOTS - 1),
+                )
+
+        build_diags(0)
+        prepare_w2()
+        build_diags(1)
+        transpose_h1(0)
+        for step in range(ROUNDS + LAG_LAYER2):
+            late = step - LAG_REGROUP
+            if step < ROUNDS:
+                h1_grouped = group_h1(step)
+            if 0 <= late < ROUNDS:
+                h2_grouped = work.tile([P, COLS, PACK], BF16, align_bytes=64)
+                for piece in range(pieces_of(late)):
+                    regroup_h2(late, h2_grouped, piece)
+            if 0 <= step - LAG_LAYER1 < ROUNDS:
+                layer1(step - LAG_LAYER1)
+            if step < ROUNDS:
+                quantise_h1(step, h1_grouped)
+            if step + 1 < ROUNDS:
+                transpose_h1(step + 1)
+            if step >= LAG_LAYER2:
+                layer2(step - LAG_LAYER2)
+            if 0 <= late < ROUNDS:
+                quantise_h2(late, h2_grouped)
+            if step + 2 < ROUNDS:
+                build_diags(step + 2)
+            if step == STEP_OF_W3:
+                prepare_w3()
+            if step == STEP_OF_BASE:
+                prepare_base()
+
+        result = keep.tile([P, NODE_BLOCKS, HID], F32)
+        for nb in range(NODE_BLOCKS):
+            nc.vector.scalar_tensor_tensor(
+                out=result[:, nb, :], in0=acc[nb][:], scalar=1.0 / SLOTS, in1=base[:, nb, :], op0=ALU.mult, op1=ALU.add
+            )
+            nc.sync.dma_start(out=out_rows[nb * P : (nb + 1) * P, :], in_=result[:, nb, :])

@@ -17,17 +17,19 @@ HID = 512
 WORDS = HID // 2
 SLOTS = 30
 NODE_BLOCKS = 2
-SLOTS_PER_ROUND = 2
-TILES = NODE_BLOCKS * SLOTS_PER_ROUND
+TILES = 4
+TILES_PER_BANK = 2
 COLS = TILES * P
-ROUNDS = SLOTS // SLOTS_PER_ROUND
+ROUNDS = NODE_BLOCKS * SLOTS // TILES
 
-LAG_LAYER1 = 1
-LAG_REGROUP = 2
-LAG_LAYER2 = 3
+LAG_LAYER1 = 2
+LAG_REGROUP = 3
+LAG_LAYER2 = 4
 STEP_OF_W3 = 0
-STEP_OF_BASE = ROUNDS - 1
-LAST_ROUND_PIECES = NODE_BLOCKS
+STEP_OF_IDLE = 1
+STEP_OF_BASE = 7
+STEP_OF_RESULT = (SLOTS // TILES + LAG_LAYER2 + 1, ROUNDS - 1 + LAG_LAYER2)
+LAST_ROUND_PIECES = 2
 
 FLOPS = 2 * 2 * (NODE_BLOCKS * P * SLOTS) * HID * HID
 
@@ -45,25 +47,37 @@ def tile_mpnnlayer_pb_kernel(tc, h1, h_V, mask_attend, W2, b2, W3, b3, out):
         work = ctx.enter_context(tc.tile_pool(name="work", bufs=3))
         psum = ctx.enter_context(tc.psum_pool(name="psum", bufs=1))
 
-        h1_sb = [keep.tile([P, SLOTS * HID], BF16, name="h1_sb%d" % nb) for nb in range(NODE_BLOCKS)]
+        h1_sb = keep.tile([P, NODE_BLOCKS * SLOTS * HID], BF16)
 
-        def load_h1(r):
-            cols = slice(r * SLOTS_PER_ROUND * HID, (r + 1) * SLOTS_PER_ROUND * HID)
-            for nb in range(NODE_BLOCKS):
-                nc.sync.dma_start(out=h1_sb[nb][:, cols], in_=h1_rows[nb * P : (nb + 1) * P, cols])
+        def load_h1(first, count):
+            nb, slot = divmod(first, SLOTS)
+            nc.sync.dma_start(
+                out=h1_sb[:, first * HID : (first + count) * HID],
+                in_=h1_rows[nb * P : (nb + 1) * P, slot * HID : (slot + count) * HID],
+            )
+
+        def load_round(r):
+            first = r * TILES
+            if first // SLOTS == (first + TILES - 1) // SLOTS:
+                load_h1(first, TILES)
+            else:
+                for half in range(2):
+                    load_h1(first + half * TILES_PER_BANK, TILES_PER_BANK)
 
         mask_bf = keep.tile([P, NODE_BLOCKS, SLOTS], BF16)
         nc.sync.dma_start(out=mask_bf[:], in_=mask_rows.rearrange("(nb q) k -> q nb k", q=P))
+        for half in range(2):
+            load_h1(half * TILES_PER_BANK, TILES_PER_BANK)
         w2_raw = keep.tile([P, PACK, HID], BF16)
         nc.sync.dma_start(out=w2_raw[:], in_=W2.rearrange("(p t) f -> p t f", t=PACK))
         b2_bf = keep.tile([P, PACK], BF16)
         nc.sync.dma_start(out=b2_bf[:], in_=b2.rearrange("(p t) -> p t", t=PACK))
-        load_h1(0)
-        load_h1(1)
+        load_round(1)
+        load_round(2)
         w3_raw = keep.tile([P, PACK, HID], BF16)
         nc.sync.dma_start(out=w3_raw[:], in_=W3.rearrange("(p t) f -> p t f", t=PACK))
-        for r in range(2, ROUNDS):
-            load_h1(r)
+        for r in range(3, ROUNDS):
+            load_round(r)
         b3_all = keep.tile([P, HID], BF16)
         nc.sync.dma_start(out=b3_all[:], in_=b3.partition_broadcast(P))
         hv = keep.tile([P, NODE_BLOCKS, HID], BF16)
@@ -71,46 +85,43 @@ def tile_mpnnlayer_pb_kernel(tc, h1, h_V, mask_attend, W2, b2, W3, b3, out):
 
         ident = keep.tile([P, P], F32)
         make_identity(nc, ident[:])
-        mask_f = keep.tile([P, ROUNDS, NODE_BLOCKS, SLOTS_PER_ROUND], F32)
-        nc.vector.tensor_copy(out=mask_f[:], in_=mask_bf[:].rearrange("q nb (r s) -> q r nb s", s=SLOTS_PER_ROUND))
-        h1_words = [h1_sb[nb][:].bitcast(F32) for nb in range(NODE_BLOCKS)]
-        diags = {}
+        masked = {}
         banks = {}
         h1_q = {}
         hiddens = {}
         h2_q = {}
 
-        def build_diags(r):
-            diag = work.tile([P, TILES, P], F32)
-            nc.vector.tensor_tensor(
-                out=diag[:],
-                in0=ident[:].unsqueeze(1).to_broadcast([P, TILES, P]),
-                in1=mask_f[:, r, :, :].rearrange("q nb s -> q (nb s)").unsqueeze(2).to_broadcast([P, TILES, P]),
-                op=ALU.mult,
-            )
-            diags[r] = diag
+        def mask_h1(r):
+            h1_masked = work.tile([P, TILES * HID], BF16)
+            for i in range(TILES):
+                tile_i = r * TILES + i
+                nc.vector.tensor_scalar(
+                    out=h1_masked[:, i * HID : (i + 1) * HID].rearrange("q (u w e) -> q u w e", u=2, e=2),
+                    in0=h1_sb[:, tile_i * HID : (tile_i + 1) * HID].rearrange("q (w u e) -> q u w e", u=2, e=2),
+                    scalar1=mask_bf[:, tile_i // SLOTS, tile_i % SLOTS : tile_i % SLOTS + 1],
+                    scalar2=None,
+                    op0=ALU.mult,
+                )
+            masked[r] = h1_masked
 
         def transpose_h1(r):
+            words = masked[r][:].bitcast(F32)
             banks[r] = []
-            for nb in range(NODE_BLOCKS):
-                bank = psum.tile([P, 2, SLOTS_PER_ROUND * P], F32, name="xt%d" % nb)
-                for s in range(SLOTS_PER_ROUND):
+            for half in range(2):
+                bank = psum.tile([P, 2, TILES_PER_BANK * P], F32, name="xt%d" % half)
+                for i in range(TILES_PER_BANK):
                     for u in range(2):
-                        first = (r * SLOTS_PER_ROUND + s) * WORDS
-                        nc.tensor.transpose(
-                            bank[:, u, s * P : (s + 1) * P],
-                            h1_words[nb][:, first + u : first + WORDS : 2],
-                            diags[r][:, nb * SLOTS_PER_ROUND + s, :],
-                        )
+                        first = (half * TILES_PER_BANK + i) * WORDS + u * P
+                        nc.tensor.transpose(bank[:, u, i * P : (i + 1) * P], words[:, first : first + P], ident[:])
                 banks[r].append(bank)
 
         def group_h1(r):
             h1_grouped = work.tile([P, COLS * PACK], BF16, align_bytes=64)
             grouped_words = h1_grouped[:].bitcast(F32).rearrange("p (c u) -> p c u", u=2)
-            for nb in range(NODE_BLOCKS):
+            for half in range(2):
                 nc.scalar.copy(
-                    out=grouped_words[:, nb * SLOTS_PER_ROUND * P : (nb + 1) * SLOTS_PER_ROUND * P, :],
-                    in_=banks[r][nb][:].rearrange("p u c -> p c u"),
+                    out=grouped_words[:, half * TILES_PER_BANK * P : (half + 1) * TILES_PER_BANK * P, :],
+                    in_=banks[r][half][:].rearrange("p u c -> p c u"),
                 )
             return h1_grouped
 
@@ -129,17 +140,21 @@ def tile_mpnnlayer_pb_kernel(tc, h1, h_V, mask_attend, W2, b2, W3, b3, out):
 
         w2_codes = keep.tile([P, HID], U32, align_bytes=64)
         w2_scales = keep.tile([P, HID], U8, align_bytes=64)
-        b2_f = keep.tile([P, PACK], F32)
+        w2_grouped = keep.tile([P, HID, PACK], BF16, align_bytes=64)
 
-        def prepare_w2():
-            nc.vector.tensor_copy(out=b2_f[:], in_=b2_bf[:])
-            w2_grouped = keep.tile([P, HID, PACK], BF16, align_bytes=64)
-            nc.vector.tensor_copy(
-                out=w2_grouped[:].rearrange("p (t2 c) t -> p t2 c t", t2=PACK),
-                in_=w2_raw[:].rearrange("p t (c t2) -> p t2 c t", t2=PACK),
+        def group_w2(copy, half):
+            blocks = slice(half * PACK // 2, (half + 1) * PACK // 2)
+            copy(
+                out=w2_grouped[:].rearrange("p (t2 c) t -> p t2 c t", t2=PACK)[:, blocks],
+                in_=w2_raw[:].rearrange("p t (c t2) -> p t2 c t", t2=PACK)[:, blocks],
             )
+
+        def quantise_w2(half):
+            cols = slice(half * HID // 2, (half + 1) * HID // 2)
             nc.vector.quantize_mx(
-                out=w2_codes[:].bitcast(FP8X4), scales=w2_scales[:], in_=w2_grouped[:].rearrange("p c t -> p (c t)")
+                out=w2_codes[:, cols].bitcast(FP8X4),
+                scales=w2_scales[:, cols],
+                in_=w2_grouped[:, cols, :].rearrange("p c t -> p (c t)"),
             )
 
         def layer1(r):
@@ -159,7 +174,7 @@ def tile_mpnnlayer_pb_kernel(tc, h1, h_V, mask_attend, W2, b2, W3, b3, out):
                         stop=True,
                     )
                     nc.scalar.activation(
-                        out=hidden[:, t2, cols], in_=x_banks[t2][:, cols], func=ACT.Relu, bias=b2_f[:, t2 : t2 + 1], scale=1.0
+                        out=hidden[:, t2, cols], in_=x_banks[t2][:, cols], func=ACT.Relu, bias=b2_bf[:, t2 : t2 + 1], scale=1.0
                     )
             hiddens[r] = hidden
 
@@ -180,27 +195,36 @@ def tile_mpnnlayer_pb_kernel(tc, h1, h_V, mask_attend, W2, b2, W3, b3, out):
                 out=w3_codes[:].bitcast(FP8X4), scales=w3_scales[:], in_=w3_grouped[:].rearrange("p f t -> p (f t)")
             )
 
+        acc = [psum.tile([P, HID], F32, name="acc%d" % nb) for nb in range(NODE_BLOCKS)]
+        kept_share = keep.tile([P, NODE_BLOCKS], F32)
+        minus_masked_share = keep.tile([P, NODE_BLOCKS], F32)
         base = keep.tile([P, NODE_BLOCKS, HID], F32)
 
-        def prepare_base():
+        idle_codes = keep.tile([P, P], U32, align_bytes=64)
+        idle_scales = keep.tile([P, P], U8, align_bytes=64)
+
+        def prepare_idle():
             idle_grouped = keep.tile([P, P, PACK], BF16, align_bytes=64)
             nc.vector.tensor_scalar(
                 out=idle_grouped[:],
-                in0=b2_f[:].unsqueeze(1).to_broadcast([P, P, PACK]),
+                in0=b2_bf[:].unsqueeze(1).to_broadcast([P, P, PACK]),
                 scalar1=0.0,
                 scalar2=None,
                 op0=ALU.max,
             )
             count = keep.tile([P, NODE_BLOCKS], F32)
-            nc.vector.reduce_sum(out=count[:], in_=mask_f[:].rearrange("q r nb s -> q nb r s"), axis=mybir.AxisListType.XY)
-            idle_codes = keep.tile([P, P], U32, align_bytes=64)
-            idle_scales = keep.tile([P, P], U8, align_bytes=64)
+            nc.vector.reduce_sum(out=count[:], in_=mask_bf[:], axis=mybir.AxisListType.X)
             nc.vector.quantize_mx(
                 out=idle_codes[:].bitcast(FP8X4), scales=idle_scales[:], in_=idle_grouped[:].rearrange("p c t -> p (c t)")
             )
-            idle_ps = psum.tile([P, HID], F32, name="xt0")
+            nc.vector.tensor_scalar(out=kept_share[:], in0=count[:], scalar1=1.0 / SLOTS, scalar2=None, op0=ALU.mult)
+            nc.vector.tensor_scalar(
+                out=minus_masked_share[:], in0=count[:], scalar1=1.0 / SLOTS, scalar2=-1.0, op0=ALU.mult, op1=ALU.add
+            )
+
+        def multiply_idle():
             nc.tensor.matmul_mx(
-                out=idle_ps[:],
+                out=acc[1][:],
                 lhsT=idle_codes[:].bitcast(FP8X4),
                 lhsT_scale=idle_scales[:],
                 rhs=w3_codes[:].bitcast(FP8X4),
@@ -208,24 +232,16 @@ def tile_mpnnlayer_pb_kernel(tc, h1, h_V, mask_attend, W2, b2, W3, b3, out):
                 start=True,
                 stop=True,
             )
-            kept_share = keep.tile([P, NODE_BLOCKS], F32)
-            nc.vector.tensor_scalar(out=kept_share[:], in0=count[:], scalar1=1.0 / SLOTS, scalar2=None, op0=ALU.mult)
-            minus_masked_share = keep.tile([P, NODE_BLOCKS], F32)
-            nc.vector.tensor_scalar(
-                out=minus_masked_share[:], in0=count[:], scalar1=1.0 / SLOTS, scalar2=-1.0, op0=ALU.mult, op1=ALU.add
-            )
-            for nb in range(NODE_BLOCKS):
-                nc.vector.scalar_tensor_tensor(
-                    out=base[:, nb, :], in0=b3_all[:], scalar=kept_share[:, nb : nb + 1], in1=hv[:, nb, :],
-                    op0=ALU.mult, op1=ALU.add,
-                )
-            for nb in range(NODE_BLOCKS):
-                nc.vector.scalar_tensor_tensor(
-                    out=base[:, nb, :], in0=idle_ps[:], scalar=minus_masked_share[:, nb : nb + 1], in1=base[:, nb, :],
-                    op0=ALU.mult, op1=ALU.add,
-                )
 
-        acc = [psum.tile([P, HID], F32, name="acc%d" % nb) for nb in range(NODE_BLOCKS)]
+        def prepare_base(nb):
+            nc.vector.scalar_tensor_tensor(
+                out=base[:, nb, :], in0=b3_all[:], scalar=kept_share[:, nb : nb + 1], in1=hv[:, nb, :],
+                op0=ALU.mult, op1=ALU.add,
+            )
+            nc.vector.scalar_tensor_tensor(
+                out=base[:, nb, :], in0=acc[1][:], scalar=minus_masked_share[:, nb : nb + 1], in1=base[:, nb, :],
+                op0=ALU.mult, op1=ALU.add,
+            )
 
         def quantise_h2(r, h2_grouped):
             h2_codes = work.tile([P, COLS], U32, align_bytes=64)
@@ -241,33 +257,47 @@ def tile_mpnnlayer_pb_kernel(tc, h1, h_V, mask_attend, W2, b2, W3, b3, out):
 
         def layer2(r):
             h2_codes, h2_scales = h2_q[r]
-            for tile_i in range(TILES):
-                slot = r * SLOTS_PER_ROUND + tile_i % SLOTS_PER_ROUND
+            for i in range(TILES):
+                nb, slot = divmod(r * TILES + i, SLOTS)
                 nc.tensor.matmul_mx(
-                    out=acc[tile_i // SLOTS_PER_ROUND][:],
-                    lhsT=h2_codes[:, tile_i * P : (tile_i + 1) * P].bitcast(FP8X4),
-                    lhsT_scale=h2_scales[:, tile_i * P : (tile_i + 1) * P],
+                    out=acc[nb][:],
+                    lhsT=h2_codes[:, i * P : (i + 1) * P].bitcast(FP8X4),
+                    lhsT_scale=h2_scales[:, i * P : (i + 1) * P],
                     rhs=w3_codes[:].bitcast(FP8X4),
                     rhs_scale=w3_scales[:],
                     start=(slot == 0),
                     stop=(slot == SLOTS - 1),
                 )
 
-        build_diags(0)
-        prepare_w2()
-        build_diags(1)
+        result = keep.tile([P, NODE_BLOCKS, HID], F32)
+
+        def finish(nb):
+            nc.vector.scalar_tensor_tensor(
+                out=result[:, nb, :], in0=acc[nb][:], scalar=1.0 / SLOTS, in1=base[:, nb, :], op0=ALU.mult, op1=ALU.add
+            )
+            nc.sync.dma_start(out=out_rows[nb * P : (nb + 1) * P, :], in_=result[:, nb, :])
+
+        mask_h1(0)
         transpose_h1(0)
+        h1_grouped = group_h1(0)
+        group_w2(nc.vector.tensor_copy, 0)
+        group_w2(nc.scalar.copy, 1)
+        quantise_w2(0)
+        quantise_h1(0, h1_grouped)
+        quantise_w2(1)
+        layer1(0)
+        mask_h1(1)
         for step in range(ROUNDS + LAG_LAYER2):
             late = step - LAG_REGROUP
-            if step < ROUNDS:
+            if 1 <= step < ROUNDS:
                 h1_grouped = group_h1(step)
             if 0 <= late < ROUNDS:
                 h2_grouped = work.tile([P, COLS, PACK], BF16, align_bytes=64)
                 for piece in range(pieces_of(late)):
                     regroup_h2(late, h2_grouped, piece)
-            if 0 <= step - LAG_LAYER1 < ROUNDS:
+            if 1 <= step - LAG_LAYER1 < ROUNDS:
                 layer1(step - LAG_LAYER1)
-            if step < ROUNDS:
+            if 1 <= step < ROUNDS:
                 quantise_h1(step, h1_grouped)
             if step + 1 < ROUNDS:
                 transpose_h1(step + 1)
@@ -276,15 +306,15 @@ def tile_mpnnlayer_pb_kernel(tc, h1, h_V, mask_attend, W2, b2, W3, b3, out):
             if 0 <= late < ROUNDS:
                 quantise_h2(late, h2_grouped)
             if step + 2 < ROUNDS:
-                build_diags(step + 2)
+                mask_h1(step + 2)
             if step == STEP_OF_W3:
                 prepare_w3()
-            if step == STEP_OF_BASE:
-                prepare_base()
-
-        result = keep.tile([P, NODE_BLOCKS, HID], F32)
-        for nb in range(NODE_BLOCKS):
-            nc.vector.scalar_tensor_tensor(
-                out=result[:, nb, :], in0=acc[nb][:], scalar=1.0 / SLOTS, in1=base[:, nb, :], op0=ALU.mult, op1=ALU.add
-            )
-            nc.sync.dma_start(out=out_rows[nb * P : (nb + 1) * P, :], in_=result[:, nb, :])
+            if step == STEP_OF_IDLE:
+                prepare_idle()
+            if step == STEP_OF_IDLE + 1:
+                multiply_idle()
+            for nb in range(NODE_BLOCKS):
+                if step == STEP_OF_BASE + nb:
+                    prepare_base(nb)
+                if step == STEP_OF_RESULT[nb]:
+                    finish(nb)

@@ -157,6 +157,12 @@ def tile_mpnnlayer_pb_kernel(tc, h1, h_V, mask_attend, W2, b2, W3, b3, out):
                 in_=w2_grouped[:, cols, :].rearrange("p c t -> p (c t)"),
             )
 
+        b2_f = keep.tile([P, PACK], F32)
+        x_of_round = {}
+
+        def blocks_of_vector(r):
+            return [PACK - 1] if r % 3 == 1 else []
+
         def layer1(r):
             codes, scales = h1_q[r]
             hidden = work.tile([P, PACK, COLS], BF16)
@@ -173,10 +179,26 @@ def tile_mpnnlayer_pb_kernel(tc, h1, h_V, mask_attend, W2, b2, W3, b3, out):
                         start=True,
                         stop=True,
                     )
+                    if t2 in blocks_of_vector(r):
+                        continue
                     nc.scalar.activation(
                         out=hidden[:, t2, cols], in_=x_banks[t2][:, cols], func=ACT.Relu, bias=b2_bf[:, t2 : t2 + 1], scale=1.0
                     )
+            x_of_round[r] = x_banks
             hiddens[r] = hidden
+
+        def layer1_on_vector(r):
+            for piece in range(pieces_of(r)):
+                cols = piece_cols(r, piece)
+                for t2 in blocks_of_vector(r):
+                    nc.vector.tensor_scalar(
+                        out=hiddens[r][:, t2, cols],
+                        in0=x_of_round[r][t2][:, cols],
+                        scalar1=b2_f[:, t2 : t2 + 1],
+                        scalar2=0.0,
+                        op0=ALU.add,
+                        op1=ALU.max,
+                    )
 
         def regroup_h2(r, h2_grouped, piece):
             cols = piece_cols(r, piece)
@@ -285,6 +307,7 @@ def tile_mpnnlayer_pb_kernel(tc, h1, h_V, mask_attend, W2, b2, W3, b3, out):
         quantise_w2(0)
         quantise_h1(0, h1_grouped)
         quantise_w2(1)
+        nc.vector.tensor_copy(out=b2_f[:], in_=b2_bf[:])
         layer1(0)
         mask_h1(1)
         for step in range(ROUNDS + LAG_LAYER2):
@@ -299,6 +322,8 @@ def tile_mpnnlayer_pb_kernel(tc, h1, h_V, mask_attend, W2, b2, W3, b3, out):
                 layer1(step - LAG_LAYER1)
             if 1 <= step < ROUNDS:
                 quantise_h1(step, h1_grouped)
+            if 1 <= step - LAG_LAYER1 < ROUNDS:
+                layer1_on_vector(step - LAG_LAYER1)
             if step + 1 < ROUNDS:
                 transpose_h1(step + 1)
             if step >= LAG_LAYER2:

@@ -22,14 +22,19 @@ TILES_PER_BANK = 2
 COLS = TILES * P
 ROUNDS = NODE_BLOCKS * SLOTS // TILES
 
-LAG_LAYER1 = 2
-LAG_REGROUP = 3
-LAG_LAYER2 = 4
+LAG_LAYER1 = 1
+LAG_REGROUP = 2
+LAG_LAYER2 = 3
 STEP_OF_W3 = 0
 STEP_OF_IDLE = 1
 STEP_OF_BASE = 7
 STEP_OF_RESULT = (SLOTS // TILES + LAG_LAYER2 + 1, ROUNDS - 1 + LAG_LAYER2)
-LAST_ROUND_PIECES = 2
+PIECES = {0: (2, 2), ROUNDS - 1: (2, 1, 1)}
+
+
+def mask_rides(r):
+    return r % 2 == 0
+
 
 FLOPS = 2 * 2 * (NODE_BLOCKS * P * SLOTS) * HID * HID
 
@@ -85,11 +90,22 @@ def tile_mpnnlayer_pb_kernel(tc, h1, h_V, mask_attend, W2, b2, W3, b3, out):
 
         ident = keep.tile([P, P], F32)
         make_identity(nc, ident[:])
+        h1_words = h1_sb[:].bitcast(F32)
+        diags = {}
         masked = {}
         banks = {}
         h1_q = {}
         hiddens = {}
         h2_q = {}
+
+        def build_diags(r):
+            diag = work.tile([P, TILES, P], F32)
+            for i in range(TILES):
+                nb, slot = divmod(r * TILES + i, SLOTS)
+                nc.vector.tensor_scalar(
+                    out=diag[:, i, :], in0=ident[:], scalar1=mask_bf[:, nb, slot : slot + 1], scalar2=None, op0=ALU.mult
+                )
+            diags[r] = diag
 
         def mask_h1(r):
             h1_masked = work.tile([P, TILES * HID], BF16)
@@ -104,15 +120,28 @@ def tile_mpnnlayer_pb_kernel(tc, h1, h_V, mask_attend, W2, b2, W3, b3, out):
                 )
             masked[r] = h1_masked
 
+        def apply_mask(r):
+            if mask_rides(r):
+                build_diags(r)
+            else:
+                mask_h1(r)
+
         def transpose_h1(r):
-            words = masked[r][:].bitcast(F32)
             banks[r] = []
             for half in range(2):
                 bank = psum.tile([P, 2, TILES_PER_BANK * P], F32, name="xt%d" % half)
                 for i in range(TILES_PER_BANK):
                     for u in range(2):
-                        first = (half * TILES_PER_BANK + i) * WORDS + u * P
-                        nc.tensor.transpose(bank[:, u, i * P : (i + 1) * P], words[:, first : first + P], ident[:])
+                        tile_of_round = half * TILES_PER_BANK + i
+                        if mask_rides(r):
+                            first = (r * TILES + tile_of_round) * WORDS
+                            words = h1_words[:, first + u : first + WORDS : 2]
+                            matrix = diags[r][:, tile_of_round, :]
+                        else:
+                            first = tile_of_round * WORDS + u * P
+                            words = masked[r][:].bitcast(F32)[:, first : first + P]
+                            matrix = ident[:]
+                        nc.tensor.transpose(bank[:, u, i * P : (i + 1) * P], words, matrix)
                 banks[r].append(bank)
 
         def group_h1(r):
@@ -125,18 +154,25 @@ def tile_mpnnlayer_pb_kernel(tc, h1, h_V, mask_attend, W2, b2, W3, b3, out):
                 )
             return h1_grouped
 
-        def quantise_h1(r, h1_grouped):
-            h1_codes = work.tile([P, COLS], U32, align_bytes=64)
-            h1_scales = work.tile([P, COLS], U8, align_bytes=64)
-            nc.vector.quantize_mx(out=h1_codes[:].bitcast(FP8X4), scales=h1_scales[:], in_=h1_grouped[:])
-            h1_q[r] = (h1_codes, h1_scales)
-
         def pieces_of(r):
-            return LAST_ROUND_PIECES if r == ROUNDS - 1 else 1
+            first, ranges = 0, []
+            for tiles in PIECES.get(r, (TILES,)):
+                ranges.append(slice(first * P, (first + tiles) * P))
+                first += tiles
+            return ranges
 
-        def piece_cols(r, piece):
-            width = COLS // pieces_of(r)
-            return slice(piece * width, (piece + 1) * width)
+        def quantise_h1(r, h1_grouped, ranges):
+            if r not in h1_q:
+                h1_codes = work.tile([P, COLS], U32, align_bytes=64)
+                h1_scales = work.tile([P, COLS], U8, align_bytes=64)
+                h1_q[r] = (h1_codes, h1_scales)
+            h1_codes, h1_scales = h1_q[r]
+            for cols in ranges:
+                nc.vector.quantize_mx(
+                    out=h1_codes[:, cols].bitcast(FP8X4),
+                    scales=h1_scales[:, cols],
+                    in_=h1_grouped[:, cols.start * PACK : cols.stop * PACK],
+                )
 
         w2_codes = keep.tile([P, HID], U32, align_bytes=64)
         w2_scales = keep.tile([P, HID], U8, align_bytes=64)
@@ -161,14 +197,13 @@ def tile_mpnnlayer_pb_kernel(tc, h1, h_V, mask_attend, W2, b2, W3, b3, out):
         x_of_round = {}
 
         def blocks_of_vector(r):
-            return [PACK - 1] if r % 3 == 1 else []
+            return [PACK - 1] if r % 4 == 1 else []
 
         def layer1(r):
             codes, scales = h1_q[r]
             hidden = work.tile([P, PACK, COLS], BF16)
             x_banks = [psum.tile([P, COLS], F32, name="x%d" % t2) for t2 in range(PACK)]
-            for piece in range(pieces_of(r)):
-                cols = piece_cols(r, piece)
+            for cols in pieces_of(r):
                 for t2 in range(PACK):
                     nc.tensor.matmul_mx(
                         out=x_banks[t2][:, cols],
@@ -188,8 +223,7 @@ def tile_mpnnlayer_pb_kernel(tc, h1, h_V, mask_attend, W2, b2, W3, b3, out):
             hiddens[r] = hidden
 
         def layer1_on_vector(r):
-            for piece in range(pieces_of(r)):
-                cols = piece_cols(r, piece)
+            for cols in pieces_of(r):
                 for t2 in blocks_of_vector(r):
                     nc.vector.tensor_scalar(
                         out=hiddens[r][:, t2, cols],
@@ -200,8 +234,7 @@ def tile_mpnnlayer_pb_kernel(tc, h1, h_V, mask_attend, W2, b2, W3, b3, out):
                         op1=ALU.max,
                     )
 
-        def regroup_h2(r, h2_grouped, piece):
-            cols = piece_cols(r, piece)
+        def regroup_h2(r, h2_grouped, cols):
             nc.vector.tensor_copy(
                 out=h2_grouped[:, cols, :].rearrange("p (c i) t -> p c t i", i=4),
                 in_=hiddens[r][:, :, cols].rearrange("p t (c i) -> p c t i", i=4),
@@ -265,17 +298,17 @@ def tile_mpnnlayer_pb_kernel(tc, h1, h_V, mask_attend, W2, b2, W3, b3, out):
                 op0=ALU.mult, op1=ALU.add,
             )
 
-        def quantise_h2(r, h2_grouped):
-            h2_codes = work.tile([P, COLS], U32, align_bytes=64)
-            h2_scales = work.tile([P, COLS], U8, align_bytes=64)
-            for piece in range(pieces_of(r)):
-                cols = piece_cols(r, piece)
-                nc.vector.quantize_mx(
-                    out=h2_codes[:, cols].bitcast(FP8X4),
-                    scales=h2_scales[:, cols],
-                    in_=h2_grouped[:, cols, :].rearrange("p c t -> p (c t)"),
-                )
-            h2_q[r] = (h2_codes, h2_scales)
+        def quantise_h2(r, h2_grouped, cols):
+            if r not in h2_q:
+                h2_codes = work.tile([P, COLS], U32, align_bytes=64)
+                h2_scales = work.tile([P, COLS], U8, align_bytes=64)
+                h2_q[r] = (h2_codes, h2_scales)
+            h2_codes, h2_scales = h2_q[r]
+            nc.vector.quantize_mx(
+                out=h2_codes[:, cols].bitcast(FP8X4),
+                scales=h2_scales[:, cols],
+                in_=h2_grouped[:, cols, :].rearrange("p c t -> p (c t)"),
+            )
 
         def layer2(r):
             h2_codes, h2_scales = h2_q[r]
@@ -299,29 +332,32 @@ def tile_mpnnlayer_pb_kernel(tc, h1, h_V, mask_attend, W2, b2, W3, b3, out):
             )
             nc.sync.dma_start(out=out_rows[nb * P : (nb + 1) * P, :], in_=result[:, nb, :])
 
-        mask_h1(0)
+        apply_mask(0)
         transpose_h1(0)
         h1_grouped = group_h1(0)
         group_w2(nc.vector.tensor_copy, 0)
         group_w2(nc.scalar.copy, 1)
         quantise_w2(0)
-        quantise_h1(0, h1_grouped)
+        quantise_h1(0, h1_grouped, pieces_of(0))
         quantise_w2(1)
         nc.vector.tensor_copy(out=b2_f[:], in_=b2_bf[:])
         layer1(0)
-        mask_h1(1)
+        apply_mask(1)
         for step in range(ROUNDS + LAG_LAYER2):
             late = step - LAG_REGROUP
             if 1 <= step < ROUNDS:
                 h1_grouped = group_h1(step)
             if 0 <= late < ROUNDS:
                 h2_grouped = work.tile([P, COLS, PACK], BF16, align_bytes=64)
-                for piece in range(pieces_of(late)):
-                    regroup_h2(late, h2_grouped, piece)
+                pieces = pieces_of(late)
+                regroup_h2(late, h2_grouped, pieces[0])
+                for done, cols in zip(pieces, pieces[1:]):
+                    regroup_h2(late, h2_grouped, cols)
+                    quantise_h2(late, h2_grouped, done)
             if 1 <= step - LAG_LAYER1 < ROUNDS:
                 layer1(step - LAG_LAYER1)
             if 1 <= step < ROUNDS:
-                quantise_h1(step, h1_grouped)
+                quantise_h1(step, h1_grouped, [slice(0, COLS)])
             if 1 <= step - LAG_LAYER1 < ROUNDS:
                 layer1_on_vector(step - LAG_LAYER1)
             if step + 1 < ROUNDS:
@@ -329,9 +365,9 @@ def tile_mpnnlayer_pb_kernel(tc, h1, h_V, mask_attend, W2, b2, W3, b3, out):
             if step >= LAG_LAYER2:
                 layer2(step - LAG_LAYER2)
             if 0 <= late < ROUNDS:
-                quantise_h2(late, h2_grouped)
+                quantise_h2(late, h2_grouped, pieces[-1])
             if step + 2 < ROUNDS:
-                mask_h1(step + 2)
+                apply_mask(step + 2)
             if step == STEP_OF_W3:
                 prepare_w3()
             if step == STEP_OF_IDLE:

@@ -20,6 +20,7 @@ NODE_BLOCKS = 2
 TILES = 4
 TILES_PER_BANK = 2
 COLS = TILES * P
+LINE = 8
 ROUNDS = NODE_BLOCKS * SLOTS // TILES
 
 LAG_LAYER1 = 1
@@ -201,7 +202,7 @@ def tile_mpnnlayer_pb_kernel(tc, h1, h_V, mask_attend, W2, b2, W3, b3, out):
 
         def layer1(r):
             codes, scales = h1_q[r]
-            hidden = work.tile([P, PACK, COLS], BF16)
+            hidden = work.tile([P, COLS // LINE, PACK, LINE], BF16, align_bytes=64)
             x_banks = [psum.tile([P, COLS], F32, name="x%d" % t2) for t2 in range(PACK)]
             for cols in pieces_of(r):
                 for t2 in range(PACK):
@@ -217,7 +218,11 @@ def tile_mpnnlayer_pb_kernel(tc, h1, h_V, mask_attend, W2, b2, W3, b3, out):
                     if t2 in blocks_of_vector(r):
                         continue
                     nc.scalar.activation(
-                        out=hidden[:, t2, cols], in_=x_banks[t2][:, cols], func=ACT.Relu, bias=b2_bf[:, t2 : t2 + 1], scale=1.0
+                        out=hidden[:, cols.start // LINE : cols.stop // LINE, t2, :],
+                        in_=x_banks[t2][:, cols].rearrange("p (b i) -> p b i", i=LINE),
+                        func=ACT.Relu,
+                        bias=b2_bf[:, t2 : t2 + 1],
+                        scale=1.0,
                     )
             x_of_round[r] = x_banks
             hiddens[r] = hidden
@@ -226,8 +231,8 @@ def tile_mpnnlayer_pb_kernel(tc, h1, h_V, mask_attend, W2, b2, W3, b3, out):
             for cols in pieces_of(r):
                 for t2 in blocks_of_vector(r):
                     nc.vector.tensor_scalar(
-                        out=hiddens[r][:, t2, cols],
-                        in0=x_of_round[r][t2][:, cols],
+                        out=hiddens[r][:, cols.start // LINE : cols.stop // LINE, t2, :],
+                        in0=x_of_round[r][t2][:, cols].rearrange("p (b i) -> p b i", i=LINE),
                         scalar1=b2_f[:, t2 : t2 + 1],
                         scalar2=0.0,
                         op0=ALU.add,
@@ -236,8 +241,8 @@ def tile_mpnnlayer_pb_kernel(tc, h1, h_V, mask_attend, W2, b2, W3, b3, out):
 
         def regroup_h2(r, h2_grouped, cols):
             nc.vector.tensor_copy(
-                out=h2_grouped[:, cols, :].rearrange("p (c i) t -> p c t i", i=4),
-                in_=hiddens[r][:, :, cols].rearrange("p t (c i) -> p c t i", i=4),
+                out=h2_grouped[:, cols, :].rearrange("p (b h i) t -> p b h t i", h=2, i=LINE // 2),
+                in_=hiddens[r][:, cols.start // LINE : cols.stop // LINE].rearrange("p b t (h i) -> p b h t i", h=2),
             )
 
         w3_codes = keep.tile([P, HID], U32, align_bytes=64)

@@ -27,15 +27,10 @@ LAG_LAYER1 = 1
 LAG_REGROUP = 2
 LAG_LAYER2 = 3
 STEP_OF_W3 = 0
-STEP_OF_IDLE = 1
+STEP_OF_IDLE = 5
 STEP_OF_BASE = 7
 STEP_OF_RESULT = (SLOTS // TILES + LAG_LAYER2 + 1, ROUNDS - 1 + LAG_LAYER2)
 PIECES = {0: (2, 2), ROUNDS - 1: (2, 1, 1)}
-
-
-def mask_rides(r):
-    return r % 2 == 0
-
 
 FLOPS = 2 * 2 * (NODE_BLOCKS * P * SLOTS) * HID * HID
 
@@ -72,17 +67,16 @@ def tile_mpnnlayer_pb_kernel(tc, h1, h_V, mask_attend, W2, b2, W3, b3, out):
 
         mask_bf = keep.tile([P, NODE_BLOCKS, SLOTS], BF16)
         nc.sync.dma_start(out=mask_bf[:], in_=mask_rows.rearrange("(nb q) k -> q nb k", q=P))
-        for half in range(2):
-            load_h1(half * TILES_PER_BANK, TILES_PER_BANK)
+        load_h1(0, TILES_PER_BANK)
         w2_raw = keep.tile([P, PACK, HID], BF16)
         nc.sync.dma_start(out=w2_raw[:], in_=W2.rearrange("(p t) f -> p t f", t=PACK))
+        load_h1(TILES_PER_BANK, TILES_PER_BANK)
         b2_bf = keep.tile([P, PACK], BF16)
         nc.sync.dma_start(out=b2_bf[:], in_=b2.rearrange("(p t) -> p t", t=PACK))
         load_round(1)
-        load_round(2)
         w3_raw = keep.tile([P, PACK, HID], BF16)
         nc.sync.dma_start(out=w3_raw[:], in_=W3.rearrange("(p t) f -> p t f", t=PACK))
-        for r in range(3, ROUNDS):
+        for r in range(2, ROUNDS):
             load_round(r)
         b3_all = keep.tile([P, HID], BF16)
         nc.sync.dma_start(out=b3_all[:], in_=b3.partition_broadcast(P))
@@ -93,8 +87,8 @@ def tile_mpnnlayer_pb_kernel(tc, h1, h_V, mask_attend, W2, b2, W3, b3, out):
         make_identity(nc, ident[:])
         h1_words = h1_sb[:].bitcast(F32)
         diags = {}
-        masked = {}
         banks = {}
+        h1_grouped = {}
         h1_q = {}
         hiddens = {}
         h2_q = {}
@@ -108,52 +102,27 @@ def tile_mpnnlayer_pb_kernel(tc, h1, h_V, mask_attend, W2, b2, W3, b3, out):
                 )
             diags[r] = diag
 
-        def mask_h1(r):
-            h1_masked = work.tile([P, TILES * HID], BF16)
-            for i in range(TILES):
-                tile_i = r * TILES + i
-                nc.vector.tensor_scalar(
-                    out=h1_masked[:, i * HID : (i + 1) * HID].rearrange("q (u w e) -> q u w e", u=2, e=2),
-                    in0=h1_sb[:, tile_i * HID : (tile_i + 1) * HID].rearrange("q (w u e) -> q u w e", u=2, e=2),
-                    scalar1=mask_bf[:, tile_i // SLOTS, tile_i % SLOTS : tile_i % SLOTS + 1],
-                    scalar2=None,
-                    op0=ALU.mult,
-                )
-            masked[r] = h1_masked
+        def transpose_h1(r, half):
+            bank = psum.tile([P, 2, TILES_PER_BANK * P], F32, name="xt%d" % half)
+            banks[r, half] = bank
+            for i in range(TILES_PER_BANK):
+                for u in range(2):
+                    tile_of_round = half * TILES_PER_BANK + i
+                    first = (r * TILES + tile_of_round) * WORDS
+                    nc.tensor.transpose(
+                        bank[:, u, i * P : (i + 1) * P],
+                        h1_words[:, first + u : first + WORDS : 2],
+                        diags[r][:, tile_of_round, :],
+                    )
 
-        def apply_mask(r):
-            if mask_rides(r):
-                build_diags(r)
-            else:
-                mask_h1(r)
-
-        def transpose_h1(r):
-            banks[r] = []
-            for half in range(2):
-                bank = psum.tile([P, 2, TILES_PER_BANK * P], F32, name="xt%d" % half)
-                for i in range(TILES_PER_BANK):
-                    for u in range(2):
-                        tile_of_round = half * TILES_PER_BANK + i
-                        if mask_rides(r):
-                            first = (r * TILES + tile_of_round) * WORDS
-                            words = h1_words[:, first + u : first + WORDS : 2]
-                            matrix = diags[r][:, tile_of_round, :]
-                        else:
-                            first = tile_of_round * WORDS + u * P
-                            words = masked[r][:].bitcast(F32)[:, first : first + P]
-                            matrix = ident[:]
-                        nc.tensor.transpose(bank[:, u, i * P : (i + 1) * P], words, matrix)
-                banks[r].append(bank)
-
-        def group_h1(r):
-            h1_grouped = work.tile([P, COLS * PACK], BF16, align_bytes=64)
-            grouped_words = h1_grouped[:].bitcast(F32).rearrange("p (c u) -> p c u", u=2)
-            for half in range(2):
-                nc.scalar.copy(
-                    out=grouped_words[:, half * TILES_PER_BANK * P : (half + 1) * TILES_PER_BANK * P, :],
-                    in_=banks[r][half][:].rearrange("p u c -> p c u"),
-                )
-            return h1_grouped
+        def group_h1(r, half):
+            if r not in h1_grouped:
+                h1_grouped[r] = work.tile([P, COLS * PACK], BF16, align_bytes=64, name="h1_grouped")
+            words = h1_grouped[r][:].bitcast(F32).rearrange("p (c u) -> p c u", u=2)
+            nc.scalar.copy(
+                out=words[:, half * TILES_PER_BANK * P : (half + 1) * TILES_PER_BANK * P, :],
+                in_=banks[r, half][:].rearrange("p u c -> p c u"),
+            )
 
         def pieces_of(r):
             first, ranges = 0, []
@@ -162,18 +131,17 @@ def tile_mpnnlayer_pb_kernel(tc, h1, h_V, mask_attend, W2, b2, W3, b3, out):
                 first += tiles
             return ranges
 
-        def quantise_h1(r, h1_grouped, ranges):
+        def quantise_h1(r, cols):
             if r not in h1_q:
                 h1_codes = work.tile([P, COLS], U32, align_bytes=64)
                 h1_scales = work.tile([P, COLS], U8, align_bytes=64)
                 h1_q[r] = (h1_codes, h1_scales)
             h1_codes, h1_scales = h1_q[r]
-            for cols in ranges:
-                nc.vector.quantize_mx(
-                    out=h1_codes[:, cols].bitcast(FP8X4),
-                    scales=h1_scales[:, cols],
-                    in_=h1_grouped[:, cols.start * PACK : cols.stop * PACK],
-                )
+            nc.vector.quantize_mx(
+                out=h1_codes[:, cols].bitcast(FP8X4),
+                scales=h1_scales[:, cols],
+                in_=h1_grouped[r][:, cols.start * PACK : cols.stop * PACK],
+            )
 
         w2_codes = keep.tile([P, HID], U32, align_bytes=64)
         w2_scales = keep.tile([P, HID], U8, align_bytes=64)
@@ -332,26 +300,33 @@ def tile_mpnnlayer_pb_kernel(tc, h1, h_V, mask_attend, W2, b2, W3, b3, out):
         result = keep.tile([P, NODE_BLOCKS, HID], F32)
 
         def finish(nb):
-            nc.vector.scalar_tensor_tensor(
-                out=result[:, nb, :], in0=acc[nb][:], scalar=1.0 / SLOTS, in1=base[:, nb, :], op0=ALU.mult, op1=ALU.add
-            )
-            nc.sync.dma_start(out=out_rows[nb * P : (nb + 1) * P, :], in_=result[:, nb, :])
+            for half in range(2):
+                cols = slice(half * HID // 2, (half + 1) * HID // 2)
+                nc.vector.scalar_tensor_tensor(
+                    out=result[:, nb, cols], in0=acc[nb][:, cols], scalar=1.0 / SLOTS, in1=base[:, nb, cols], op0=ALU.mult, op1=ALU.add
+                )
+                nc.sync.dma_start(out=out_rows[nb * P : (nb + 1) * P, cols], in_=result[:, nb, cols])
 
-        apply_mask(0)
-        transpose_h1(0)
-        h1_grouped = group_h1(0)
+        build_diags(0)
+        first_half, second_half = pieces_of(0)
+        transpose_h1(0, 0)
+        group_h1(0, 0)
         group_w2(nc.vector.tensor_copy, 0)
         group_w2(nc.scalar.copy, 1)
+        transpose_h1(0, 1)
+        group_h1(0, 1)
         quantise_w2(0)
-        quantise_h1(0, h1_grouped, pieces_of(0))
+        quantise_h1(0, first_half)
         quantise_w2(1)
+        quantise_h1(0, second_half)
         nc.vector.tensor_copy(out=b2_f[:], in_=b2_bf[:])
         layer1(0)
-        apply_mask(1)
+        build_diags(1)
         for step in range(ROUNDS + LAG_LAYER2):
             late = step - LAG_REGROUP
             if 1 <= step < ROUNDS:
-                h1_grouped = group_h1(step)
+                for half in range(2):
+                    group_h1(step, half)
             if 0 <= late < ROUNDS:
                 h2_grouped = work.tile([P, COLS, PACK], BF16, align_bytes=64)
                 pieces = pieces_of(late)
@@ -362,17 +337,18 @@ def tile_mpnnlayer_pb_kernel(tc, h1, h_V, mask_attend, W2, b2, W3, b3, out):
             if 1 <= step - LAG_LAYER1 < ROUNDS:
                 layer1(step - LAG_LAYER1)
             if 1 <= step < ROUNDS:
-                quantise_h1(step, h1_grouped, [slice(0, COLS)])
+                quantise_h1(step, slice(0, COLS))
             if 1 <= step - LAG_LAYER1 < ROUNDS:
                 layer1_on_vector(step - LAG_LAYER1)
             if step + 1 < ROUNDS:
-                transpose_h1(step + 1)
+                for half in range(2):
+                    transpose_h1(step + 1, half)
             if step >= LAG_LAYER2:
                 layer2(step - LAG_LAYER2)
             if 0 <= late < ROUNDS:
                 quantise_h2(late, h2_grouped, pieces[-1])
             if step + 2 < ROUNDS:
-                apply_mask(step + 2)
+                build_diags(step + 2)
             if step == STEP_OF_W3:
                 prepare_w3()
             if step == STEP_OF_IDLE:

@@ -26,11 +26,10 @@ ROUNDS = NODE_BLOCKS * SLOTS // TILES
 LAG_LAYER1 = 1
 LAG_REGROUP = 2
 LAG_LAYER2 = 3
-STEP_OF_W3 = 0
 STEP_OF_IDLE = 5
 STEP_OF_BASE = 7
-STEP_OF_RESULT = (SLOTS // TILES + LAG_LAYER2 + 1, ROUNDS - 1 + LAG_LAYER2)
-PIECES = {0: (2, 2), ROUNDS - 1: (2, 1, 1)}
+STEP_OF_RESULT = (SLOTS // TILES + LAG_LAYER2 + 1, ROUNDS + LAG_LAYER2)
+PIECES = {ROUNDS - 2: (2, 2), ROUNDS - 1: (2, 1, 1)}
 
 FLOPS = 2 * 2 * (NODE_BLOCKS * P * SLOTS) * HID * HID
 
@@ -67,10 +66,10 @@ def tile_mpnnlayer_pb_kernel(tc, h1, h_V, mask_attend, W2, b2, W3, b3, out):
 
         mask_bf = keep.tile([P, NODE_BLOCKS, SLOTS], BF16)
         nc.sync.dma_start(out=mask_bf[:], in_=mask_rows.rearrange("(nb q) k -> q nb k", q=P))
-        load_h1(0, TILES_PER_BANK)
+        for half in range(2):
+            load_h1(half * TILES_PER_BANK, TILES_PER_BANK)
         w2_raw = keep.tile([P, PACK, HID], BF16)
         nc.sync.dma_start(out=w2_raw[:], in_=W2.rearrange("(p t) f -> p t f", t=PACK))
-        load_h1(TILES_PER_BANK, TILES_PER_BANK)
         b2_bf = keep.tile([P, PACK], BF16)
         nc.sync.dma_start(out=b2_bf[:], in_=b2.rearrange("(p t) -> p t", t=PACK))
         load_round(1)
@@ -103,7 +102,7 @@ def tile_mpnnlayer_pb_kernel(tc, h1, h_V, mask_attend, W2, b2, W3, b3, out):
             diags[r] = diag
 
         def transpose_h1(r, half):
-            bank = psum.tile([P, 2, TILES_PER_BANK * P], F32, name="xt%d" % half)
+            bank = psum.tile([P, 2, TILES_PER_BANK * P], F32, name=("acc%d" if r == 1 else "xt%d") % half)
             banks[r, half] = bank
             for i in range(TILES_PER_BANK):
                 for u in range(2):
@@ -168,7 +167,7 @@ def tile_mpnnlayer_pb_kernel(tc, h1, h_V, mask_attend, W2, b2, W3, b3, out):
         def blocks_of_vector(r):
             return [PACK - 1] if r % 4 == 1 else []
 
-        def layer1(r):
+        def layer1(r, woven=None):
             codes, scales = h1_q[r]
             hidden = work.tile([P, COLS // LINE, PACK, LINE], BF16, align_bytes=64)
             x_banks = [psum.tile([P, COLS], F32, name="x%d" % t2) for t2 in range(PACK)]
@@ -183,6 +182,8 @@ def tile_mpnnlayer_pb_kernel(tc, h1, h_V, mask_attend, W2, b2, W3, b3, out):
                         start=True,
                         stop=True,
                     )
+                    if woven is not None and cols.start == 0:
+                        layer2(woven, t2)
                     if t2 in blocks_of_vector(r):
                         continue
                     nc.scalar.activation(
@@ -223,7 +224,7 @@ def tile_mpnnlayer_pb_kernel(tc, h1, h_V, mask_attend, W2, b2, W3, b3, out):
                 out=w3_codes[:].bitcast(FP8X4), scales=w3_scales[:], in_=w3_grouped[:].rearrange("p f t -> p (f t)")
             )
 
-        acc = [psum.tile([P, HID], F32, name="acc%d" % nb) for nb in range(NODE_BLOCKS)]
+        acc = []
         kept_share = keep.tile([P, NODE_BLOCKS], F32)
         minus_masked_share = keep.tile([P, NODE_BLOCKS], F32)
         base = keep.tile([P, NODE_BLOCKS, HID], F32)
@@ -283,19 +284,18 @@ def tile_mpnnlayer_pb_kernel(tc, h1, h_V, mask_attend, W2, b2, W3, b3, out):
                 in_=h2_grouped[:, cols, :].rearrange("p c t -> p (c t)"),
             )
 
-        def layer2(r):
+        def layer2(r, i):
             h2_codes, h2_scales = h2_q[r]
-            for i in range(TILES):
-                nb, slot = divmod(r * TILES + i, SLOTS)
-                nc.tensor.matmul_mx(
-                    out=acc[nb][:],
-                    lhsT=h2_codes[:, i * P : (i + 1) * P].bitcast(FP8X4),
-                    lhsT_scale=h2_scales[:, i * P : (i + 1) * P],
-                    rhs=w3_codes[:].bitcast(FP8X4),
-                    rhs_scale=w3_scales[:],
-                    start=(slot == 0),
-                    stop=(slot == SLOTS - 1),
-                )
+            nb, slot = divmod(r * TILES + i, SLOTS)
+            nc.tensor.matmul_mx(
+                out=acc[nb][:],
+                lhsT=h2_codes[:, i * P : (i + 1) * P].bitcast(FP8X4),
+                lhsT_scale=h2_scales[:, i * P : (i + 1) * P],
+                rhs=w3_codes[:].bitcast(FP8X4),
+                rhs_scale=w3_scales[:],
+                start=(slot == 0),
+                stop=(slot == SLOTS - 1),
+            )
 
         result = keep.tile([P, NODE_BLOCKS, HID], F32)
 
@@ -308,23 +308,26 @@ def tile_mpnnlayer_pb_kernel(tc, h1, h_V, mask_attend, W2, b2, W3, b3, out):
                 nc.sync.dma_start(out=out_rows[nb * P : (nb + 1) * P, cols], in_=result[:, nb, cols])
 
         build_diags(0)
-        first_half, second_half = pieces_of(0)
-        transpose_h1(0, 0)
-        group_h1(0, 0)
+        build_diags(1)
+        for half in range(2):
+            transpose_h1(0, half)
+            group_h1(0, half)
         group_w2(nc.vector.tensor_copy, 0)
         group_w2(nc.scalar.copy, 1)
-        transpose_h1(0, 1)
-        group_h1(0, 1)
         quantise_w2(0)
-        quantise_h1(0, first_half)
+        quantise_h1(0, slice(0, COLS))
         quantise_w2(1)
-        quantise_h1(0, second_half)
         nc.vector.tensor_copy(out=b2_f[:], in_=b2_bf[:])
+        for half in range(2):
+            transpose_h1(1, half)
+        for half in range(2):
+            group_h1(1, half)
         layer1(0)
-        build_diags(1)
-        for step in range(ROUNDS + LAG_LAYER2):
+        build_diags(2)
+        prepare_w3()
+        for step in range(1, ROUNDS + LAG_LAYER2 + 1):
             late = step - LAG_REGROUP
-            if 1 <= step < ROUNDS:
+            if 2 <= step < ROUNDS:
                 for half in range(2):
                     group_h1(step, half)
             if 0 <= late < ROUNDS:
@@ -334,23 +337,28 @@ def tile_mpnnlayer_pb_kernel(tc, h1, h_V, mask_attend, W2, b2, W3, b3, out):
                 for done, cols in zip(pieces, pieces[1:]):
                     regroup_h2(late, h2_grouped, cols)
                     quantise_h2(late, h2_grouped, done)
+            weave = step >= ROUNDS - 1 and step - LAG_LAYER1 < ROUNDS
+            behind = LAG_LAYER2 if step < ROUNDS - 2 else LAG_LAYER2 + 1
             if 1 <= step - LAG_LAYER1 < ROUNDS:
-                layer1(step - LAG_LAYER1)
-            if 1 <= step < ROUNDS:
+                layer1(step - LAG_LAYER1, step - behind if weave else None)
+            if step < ROUNDS:
                 quantise_h1(step, slice(0, COLS))
             if 1 <= step - LAG_LAYER1 < ROUNDS:
                 layer1_on_vector(step - LAG_LAYER1)
             if step + 1 < ROUNDS:
                 for half in range(2):
                     transpose_h1(step + 1, half)
-            if step >= LAG_LAYER2:
-                layer2(step - LAG_LAYER2)
+            if step == LAG_LAYER2:
+                for nb in range(NODE_BLOCKS):
+                    bank = psum.tile([P, HID], F32, name="acc%d" % nb)
+                    acc.append(bank)
+            if step >= LAG_LAYER2 and not weave and step != ROUNDS - 2:
+                for i in range(TILES):
+                    layer2(step - behind, i)
             if 0 <= late < ROUNDS:
                 quantise_h2(late, h2_grouped, pieces[-1])
             if step + 2 < ROUNDS:
                 build_diags(step + 2)
-            if step == STEP_OF_W3:
-                prepare_w3()
             if step == STEP_OF_IDLE:
                 prepare_idle()
             if step == STEP_OF_IDLE + 1:

from contextlib import ExitStack

import concourse.mybir as mybir
from concourse.masks import make_identity

F32 = mybir.dt.float32
BF16 = mybir.dt.bfloat16
U32 = mybir.dt.uint32
U8 = mybir.dt.uint8
FP8X4 = mybir.dt.float8_e4m3fn_x4
ALU = mybir.AluOpType
ACT = mybir.ActivationFunctionType

P = 128
PACK = 4
HID = 512
WORDS = HID // 2
SLOTS = 30
NODE_BLOCKS = 2
TILES = 4
TILES_PER_BANK = 2
COLS = TILES * P
LINE = 8
ROUNDS = NODE_BLOCKS * SLOTS // TILES

LAG_LAYER1 = 1
LAG_REGROUP = 2
LAG_LAYER2 = 3
STEP_OF_IDLE = 5
STEP_OF_BASE = 7
STEP_OF_RESULT = (SLOTS // TILES + LAG_LAYER2 + 1, ROUNDS + LAG_LAYER2)
PIECES = {ROUNDS - 2: (2, 2), ROUNDS - 1: (2, 1, 1)}

FLOPS = 2 * 2 * (NODE_BLOCKS * P * SLOTS) * HID * HID


def tile_mpnnlayer_pb_kernel(tc, h1, h_V, mask_attend, W2, b2, W3, b3, out):
    nc = tc.nc
    h1_rows = h1.rearrange("b n k h -> (b n) (k h)")
    hv_rows = h_V.rearrange("b n h -> (b n) h")
    mask_rows = mask_attend.rearrange("b n k -> (b n) k")
    out_rows = out.rearrange("b n h -> (b n) h")

    with ExitStack() as ctx:
        ctx.enter_context(tc.manual_schedule())
        keep = ctx.enter_context(tc.tile_pool(name="keep", bufs=1))
        work = ctx.enter_context(tc.tile_pool(name="work", bufs=3))
        psum = ctx.enter_context(tc.psum_pool(name="psum", bufs=1))

        h1_sb = keep.tile([P, NODE_BLOCKS * SLOTS * HID], BF16)

        def load_h1(first, count):
            nb, slot = divmod(first, SLOTS)
            nc.sync.dma_start(
                out=h1_sb[:, first * HID : (first + count) * HID],
                in_=h1_rows[nb * P : (nb + 1) * P, slot * HID : (slot + count) * HID],
            )

        def load_round(r):
            first = r * TILES
            if first // SLOTS == (first + TILES - 1) // SLOTS:
                load_h1(first, TILES)
            else:
                for half in range(2):
                    load_h1(first + half * TILES_PER_BANK, TILES_PER_BANK)

        mask_bf = keep.tile([P, NODE_BLOCKS, SLOTS], BF16)
        nc.sync.dma_start(out=mask_bf[:], in_=mask_rows.rearrange("(nb q) k -> q nb k", q=P))
        for half in range(2):
            load_h1(half * TILES_PER_BANK, TILES_PER_BANK)
        w2_raw = keep.tile([P, PACK, HID], BF16)
        nc.sync.dma_start(out=w2_raw[:], in_=W2.rearrange("(p t) f -> p t f", t=PACK))
        b2_bf = keep.tile([P, PACK], BF16)
        nc.sync.dma_start(out=b2_bf[:], in_=b2.rearrange("(p t) -> p t", t=PACK))
        load_round(1)
        w3_raw = keep.tile([P, PACK, HID], BF16)
        nc.sync.dma_start(out=w3_raw[:], in_=W3.rearrange("(p t) f -> p t f", t=PACK))
        for r in range(2, ROUNDS):
            load_round(r)
        b3_all = keep.tile([P, HID], BF16)
        nc.sync.dma_start(out=b3_all[:], in_=b3.partition_broadcast(P))
        hv = keep.tile([P, NODE_BLOCKS, HID], BF16)
        nc.sync.dma_start(out=hv[:], in_=hv_rows.rearrange("(nb q) h -> q nb h", q=P))

        ident = keep.tile([P, P], F32)
        make_identity(nc, ident[:])
        h1_words = h1_sb[:].bitcast(F32)
        diags = {}
        banks = {}
        h1_grouped = {}
        h1_q = {}
        hiddens = {}
        h2_q = {}

        def build_diags(r):
            diag = work.tile([P, TILES, P], F32)
            for i in range(TILES):
                nb, slot = divmod(r * TILES + i, SLOTS)
                nc.vector.tensor_scalar(
                    out=diag[:, i, :], in0=ident[:], scalar1=mask_bf[:, nb, slot : slot + 1], scalar2=None, op0=ALU.mult
                )
            diags[r] = diag

        def transpose_h1(r, half):
            bank = psum.tile([P, 2, TILES_PER_BANK * P], F32, name=("acc%d" if r == 1 else "xt%d") % half)
            banks[r, half] = bank
            for i in range(TILES_PER_BANK):
                for u in range(2):
                    tile_of_round = half * TILES_PER_BANK + i
                    first = (r * TILES + tile_of_round) * WORDS
                    nc.tensor.transpose(
                        bank[:, u, i * P : (i + 1) * P],
                        h1_words[:, first + u : first + WORDS : 2],
                        diags[r][:, tile_of_round, :],
                    )

        def group_h1(r, half):
            if r not in h1_grouped:
                h1_grouped[r] = work.tile([P, COLS * PACK], BF16, align_bytes=64, name="h1_grouped")
            words = h1_grouped[r][:].bitcast(F32).rearrange("p (c u) -> p c u", u=2)
            nc.scalar.copy(
                out=words[:, half * TILES_PER_BANK * P : (half + 1) * TILES_PER_BANK * P, :],
                in_=banks[r, half][:].rearrange("p u c -> p c u"),
            )

        def pieces_of(r):
            first, ranges = 0, []
            for tiles in PIECES.get(r, (TILES,)):
                ranges.append(slice(first * P, (first + tiles) * P))
                first += tiles
            return ranges

        def quantise_h1(r, cols):
            if r not in h1_q:
                h1_codes = work.tile([P, COLS], U32, align_bytes=64)
                h1_scales = work.tile([P, COLS], U8, align_bytes=64)
                h1_q[r] = (h1_codes, h1_scales)
            h1_codes, h1_scales = h1_q[r]
            nc.vector.quantize_mx(
                out=h1_codes[:, cols].bitcast(FP8X4),
                scales=h1_scales[:, cols],
                in_=h1_grouped[r][:, cols.start * PACK : cols.stop * PACK],
            )

        w2_codes = keep.tile([P, HID], U32, align_bytes=64)
        w2_scales = keep.tile([P, HID], U8, align_bytes=64)
        w2_grouped = keep.tile([P, HID, PACK], BF16, align_bytes=64)

        def group_w2(copy, half):
            blocks = slice(half * PACK // 2, (half + 1) * PACK // 2)
            copy(
                out=w2_grouped[:].rearrange("p (t2 c) t -> p t2 c t", t2=PACK)[:, blocks],
                in_=w2_raw[:].rearrange("p t (c t2) -> p t2 c t", t2=PACK)[:, blocks],
            )

        def quantise_w2(half):
            cols = slice(half * HID // 2, (half + 1) * HID // 2)
            nc.vector.quantize_mx(
                out=w2_codes[:, cols].bitcast(FP8X4),
                scales=w2_scales[:, cols],
                in_=w2_grouped[:, cols, :].rearrange("p c t -> p (c t)"),
            )

        b2_f = keep.tile([P, PACK], F32)
        x_of_round = {}

        def blocks_of_vector(r):
            return [PACK - 1] if r % 4 == 1 else []

        def layer1(r, woven=None):
            codes, scales = h1_q[r]
            hidden = work.tile([P, COLS // LINE, PACK, LINE], BF16, align_bytes=64)
            x_banks = [psum.tile([P, COLS], F32, name="x%d" % t2) for t2 in range(PACK)]
            for cols in pieces_of(r):
                for t2 in range(PACK):
                    nc.tensor.matmul_mx(
                        out=x_banks[t2][:, cols],
                        lhsT=w2_codes[:, t2 * P : (t2 + 1) * P].bitcast(FP8X4),
                        lhsT_scale=w2_scales[:, t2 * P : (t2 + 1) * P],
                        rhs=codes[:, cols].bitcast(FP8X4),
                        rhs_scale=scales[:, cols],
                        start=True,
                        stop=True,
                    )
                    if woven is not None and cols.start == 0:
                        layer2(woven, t2)
                    if t2 in blocks_of_vector(r):
                        continue
                    nc.scalar.activation(
                        out=hidden[:, cols.start // LINE : cols.stop // LINE, t2, :],
                        in_=x_banks[t2][:, cols].rearrange("p (b i) -> p b i", i=LINE),
                        func=ACT.Relu,
                        bias=b2_bf[:, t2 : t2 + 1],
                        scale=1.0,
                    )
            x_of_round[r] = x_banks
            hiddens[r] = hidden

        def layer1_on_vector(r):
            for cols in pieces_of(r):
                for t2 in blocks_of_vector(r):
                    nc.vector.tensor_scalar(
                        out=hiddens[r][:, cols.start // LINE : cols.stop // LINE, t2, :],
                        in0=x_of_round[r][t2][:, cols].rearrange("p (b i) -> p b i", i=LINE),
                        scalar1=b2_f[:, t2 : t2 + 1],
                        scalar2=0.0,
                        op0=ALU.add,
                        op1=ALU.max,
                    )

        def regroup_h2(r, h2_grouped, cols):
            nc.vector.tensor_copy(
                out=h2_grouped[:, cols, :].rearrange("p (b h i) t -> p b h t i", h=2, i=LINE // 2),
                in_=hiddens[r][:, cols.start // LINE : cols.stop // LINE].rearrange("p b t (h i) -> p b h t i", h=2),
            )

        w3_codes = keep.tile([P, HID], U32, align_bytes=64)
        w3_scales = keep.tile([P, HID], U8, align_bytes=64)

        def prepare_w3():
            w3_grouped = keep.tile([P, HID, PACK], BF16, align_bytes=64)
            nc.vector.tensor_copy(out=w3_grouped[:], in_=w3_raw[:].rearrange("p t f -> p f t"))
            nc.vector.quantize_mx(
                out=w3_codes[:].bitcast(FP8X4), scales=w3_scales[:], in_=w3_grouped[:].rearrange("p f t -> p (f t)")
            )

        acc = []
        kept_share = keep.tile([P, NODE_BLOCKS], F32)
        minus_masked_share = keep.tile([P, NODE_BLOCKS], F32)
        base = keep.tile([P, NODE_BLOCKS, HID], F32)

        idle_codes = keep.tile([P, P], U32, align_bytes=64)
        idle_scales = keep.tile([P, P], U8, align_bytes=64)

        def prepare_idle():
            idle_grouped = keep.tile([P, P, PACK], BF16, align_bytes=64)
            nc.vector.tensor_scalar(
                out=idle_grouped[:],
                in0=b2_bf[:].unsqueeze(1).to_broadcast([P, P, PACK]),
                scalar1=0.0,
                scalar2=None,
                op0=ALU.max,
            )
            count = keep.tile([P, NODE_BLOCKS], F32)
            nc.vector.reduce_sum(out=count[:], in_=mask_bf[:], axis=mybir.AxisListType.X)
            nc.vector.quantize_mx(
                out=idle_codes[:].bitcast(FP8X4), scales=idle_scales[:], in_=idle_grouped[:].rearrange("p c t -> p (c t)")
            )
            nc.vector.tensor_scalar(out=kept_share[:], in0=count[:], scalar1=1.0 / SLOTS, scalar2=None, op0=ALU.mult)
            nc.vector.tensor_scalar(
                out=minus_masked_share[:], in0=count[:], scalar1=1.0 / SLOTS, scalar2=-1.0, op0=ALU.mult, op1=ALU.add
            )

        def multiply_idle():
            nc.tensor.matmul_mx(
                out=acc[1][:],
                lhsT=idle_codes[:].bitcast(FP8X4),
                lhsT_scale=idle_scales[:],
                rhs=w3_codes[:].bitcast(FP8X4),
                rhs_scale=w3_scales[:],
                start=True,
                stop=True,
            )

        def prepare_base(nb):
            nc.vector.scalar_tensor_tensor(
                out=base[:, nb, :], in0=b3_all[:], scalar=kept_share[:, nb : nb + 1], in1=hv[:, nb, :],
                op0=ALU.mult, op1=ALU.add,
            )
            nc.vector.scalar_tensor_tensor(
                out=base[:, nb, :], in0=acc[1][:], scalar=minus_masked_share[:, nb : nb + 1], in1=base[:, nb, :],
                op0=ALU.mult, op1=ALU.add,
            )

        def quantise_h2(r, h2_grouped, cols):
            if r not in h2_q:
                h2_codes = work.tile([P, COLS], U32, align_bytes=64)
                h2_scales = work.tile([P, COLS], U8, align_bytes=64)
                h2_q[r] = (h2_codes, h2_scales)
            h2_codes, h2_scales = h2_q[r]
            nc.vector.quantize_mx(
                out=h2_codes[:, cols].bitcast(FP8X4),
                scales=h2_scales[:, cols],
                in_=h2_grouped[:, cols, :].rearrange("p c t -> p (c t)"),
            )

        def layer2(r, i):
            h2_codes, h2_scales = h2_q[r]
            nb, slot = divmod(r * TILES + i, SLOTS)
            nc.tensor.matmul_mx(
                out=acc[nb][:],
                lhsT=h2_codes[:, i * P : (i + 1) * P].bitcast(FP8X4),
                lhsT_scale=h2_scales[:, i * P : (i + 1) * P],
                rhs=w3_codes[:].bitcast(FP8X4),
                rhs_scale=w3_scales[:],
                start=(slot == 0),
                stop=(slot == SLOTS - 1),
            )

        result = keep.tile([P, NODE_BLOCKS, HID], F32)

        def finish(nb):
            for half in range(2):
                cols = slice(half * HID // 2, (half + 1) * HID // 2)
                nc.vector.scalar_tensor_tensor(
                    out=result[:, nb, cols], in0=acc[nb][:, cols], scalar=1.0 / SLOTS, in1=base[:, nb, cols], op0=ALU.mult, op1=ALU.add
                )
                nc.sync.dma_start(out=out_rows[nb * P : (nb + 1) * P, cols], in_=result[:, nb, cols])

        build_diags(0)
        build_diags(1)
        for half in range(2):
            transpose_h1(0, half)
            group_h1(0, half)
        group_w2(nc.vector.tensor_copy, 0)
        group_w2(nc.scalar.copy, 1)
        quantise_w2(0)
        quantise_h1(0, slice(0, COLS))
        quantise_w2(1)
        nc.vector.tensor_copy(out=b2_f[:], in_=b2_bf[:])
        for half in range(2):
            transpose_h1(1, half)
        for half in range(2):
            group_h1(1, half)
        layer1(0)
        build_diags(2)
        prepare_w3()
        for step in range(1, ROUNDS + LAG_LAYER2 + 1):
            late = step - LAG_REGROUP
            if 2 <= step < ROUNDS:
                for half in range(2):
                    group_h1(step, half)
            if 0 <= late < ROUNDS:
                h2_grouped = work.tile([P, COLS, PACK], BF16, align_bytes=64)
                pieces = pieces_of(late)
                regroup_h2(late, h2_grouped, pieces[0])
                for done, cols in zip(pieces, pieces[1:]):
                    regroup_h2(late, h2_grouped, cols)
                    quantise_h2(late, h2_grouped, done)
            weave = step >= ROUNDS - 1 and step - LAG_LAYER1 < ROUNDS
            behind = LAG_LAYER2 if step < ROUNDS - 2 else LAG_LAYER2 + 1
            if 1 <= step - LAG_LAYER1 < ROUNDS:
                layer1(step - LAG_LAYER1, step - behind if weave else None)
            if step < ROUNDS:
                quantise_h1(step, slice(0, COLS))
            if 1 <= step - LAG_LAYER1 < ROUNDS:
                layer1_on_vector(step - LAG_LAYER1)
            if step + 1 < ROUNDS:
                for half in range(2):
                    transpose_h1(step + 1, half)
            if step == LAG_LAYER2:
                for nb in range(NODE_BLOCKS):
                    bank = psum.tile([P, HID], F32, name="acc%d" % nb)
                    acc.append(bank)
            if step >= LAG_LAYER2 and not weave and step != ROUNDS - 2:
                for i in range(TILES):
                    layer2(step - behind, i)
            if 0 <= late < ROUNDS:
                quantise_h2(late, h2_grouped, pieces[-1])
            if step + 2 < ROUNDS:
                build_diags(step + 2)
            if step == STEP_OF_IDLE:
                prepare_idle()
            if step == STEP_OF_IDLE + 1:
                multiply_idle()
            for nb in range(NODE_BLOCKS):
                if step == STEP_OF_BASE + nb:
                    prepare_base(nb)
                if step == STEP_OF_RESULT[nb]:
                    finish(nb)
